import numpy as np
import ml_dtypes


def mxq(x, axis, fmt="e4m3"):
    dtype, down = {"e4m3": (ml_dtypes.float8_e4m3fn, 7), "e5m2": (ml_dtypes.float8_e5m2, 14)}[fmt]
    v = np.moveaxis(np.asarray(x, np.float32).astype(ml_dtypes.bfloat16).astype(np.float64), axis, -1)
    blocks = v.reshape(v.shape[:-1] + (-1, 32))
    amax = np.abs(blocks).max(-1, keepdims=True)
    byte = np.maximum(np.where(amax > 0, np.frexp(amax)[1] - 1 + 127, 0) - down, 1)
    scale = np.exp2(byte - 127.0)
    codes = (blocks / scale).astype(np.float32).astype(dtype).astype(np.float64)
    return np.moveaxis((codes * scale).reshape(v.shape), -1, axis)


WIDE = False


def mx_kscale(k):
    if not WIDE:
        return np.ones(k)
    levels = np.array([10, -10, 5, -5, 0])
    if k % 512:
        return np.exp2(np.random.permutation(np.resize(levels, k // 32))).repeat(32)
    a = np.empty((k // 512, 16))
    for p in range(k // 512):
        a[p, :8] = np.random.permutation(np.resize(levels, 8))
        for g in range(8):
            far = levels[np.abs(levels - a[p, g]) >= 10]
            a[p, g + 8] = far[np.random.randint(len(far))]
    return np.exp2(a.ravel()).repeat(32)


BF16 = ml_dtypes.bfloat16


def bf(x):
    return np.asarray(x, np.float32).astype(BF16)


def f64(x):
    return np.asarray(x).astype(np.float64)


B, S, IN_DIM, UNITS = 8, 2048, 512, 128
EPS = 1e-6


def _ternary_kernel():
    limit = np.sqrt(6.0 / (IN_DIM + UNITS))
    w = np.random.uniform(-limit, limit, (IN_DIM, UNITS))
    scale = np.mean(np.abs(w)) + EPS
    return np.clip(np.round(w / scale), -1.0, 1.0)


def setup_inputs():
    s = mx_kscale(IN_DIM)
    return {"x": bf(np.random.standard_normal((B, S, IN_DIM)) * (1.2 / np.sqrt(IN_DIM)) * s),
            "kernel": bf(_ternary_kernel() / s[:, None]),
            "bias": bf(np.random.standard_normal(UNITS) * 0.1)}


def reference(x, kernel, bias):
    return (mxq(f64(x), 2, "e4m3") @ mxq(f64(kernel), 0, "e4m3")) + f64(bias)

@@ -1,0 +1,176 @@
+from contextlib import ExitStack
+
+import concourse.bass as bass
+import concourse.mybir as mybir
+import concourse.tile as tile
+from concourse.masks import make_identity
+
+F32 = mybir.dt.float32
+BF16 = mybir.dt.bfloat16
+U32 = mybir.dt.uint32
+U8 = mybir.dt.uint8
+FP8X4 = mybir.dt.float8_e4m3fn_x4
+
+P = 128
+TOKENS = 8 * 2048
+D = 512
+UNITS = 128
+FLOPS = 2 * TOKENS * D * UNITS
+
+LOADS = [4, 4, 8, 16, 16, 16, 16, 16, 16, 16]
+STORES = [64, 32, 16, 8, 8]
+TILES = TOKENS // P
+GROUP = 4
+RUN = 2
+T_BANKS = 5
+O_BANKS = 3
+
+
+def tile_bitlinear_t_kernel(tc, x, kernel, bias, out):
+    nc = tc.nc
+    xf = x.flatten_outer_dims().rearrange("(p t) d -> p (t d)", t=TILES)
+    of = out.flatten_outer_dims().rearrange("(p t) u -> p (t u)", t=TILES)
+    assert sum(LOADS) == TILES and sum(STORES) == TILES
+
+    with ExitStack() as ctx:
+        ctx.enter_context(tc.manual_schedule())
+        const = ctx.enter_context(tc.tile_pool(name="const", bufs=1))
+        xin = ctx.enter_context(tc.tile_pool(name="xin", bufs=1))
+        res = ctx.enter_context(tc.tile_pool(name="res", bufs=1))
+        stage = ctx.enter_context(tc.tile_pool(name="stage", bufs=4))
+        tps = ctx.enter_context(tc.psum_pool(name="tps", bufs=T_BANKS))
+        ops = ctx.enter_context(tc.psum_pool(name="ops", bufs=O_BANKS))
+
+        wraw = const.tile([P, 4, UNITS], BF16, name="wraw")
+        nc.scalar.dma_start(out=wraw[:], in_=kernel.rearrange("(p j) c -> p j c", j=4))
+        brow = const.tile([P, UNITS], BF16, name="brow")
+        nc.vector.memset(brow[:], 0.0)
+        nc.scalar.dma_start(out=brow[0:1, :], in_=bias.rearrange("(o u) -> o u", o=1))
+        ones = const.tile([P, P], BF16, name="ones")
+        nc.vector.memset(ones[:], 1.0)
+        ident = const.tile([P, P], F32, name="ident")
+        make_identity(nc, ident[:])
+
+        x_tiles = []
+        where = []
+        first = 0
+        for ci, width in enumerate(LOADS):
+            xc = xin.tile([P, width * D], BF16, name="x%d" % ci)
+            nc.sync.dma_start(out=xc[:], in_=xf[:, first * D : (first + width) * D])
+            x_tiles.append(xc)
+            for t0 in range(0, width, GROUP):
+                where.append((ci, t0))
+            first += width
+        o_tiles = []
+        where_out = []
+        first = 0
+        for ci, width in enumerate(STORES):
+            oc = res.tile([P, width * UNITS], F32, name="o%d" % ci)
+            o_tiles.append((oc, first, width))
+            for t0 in range(0, width, GROUP):
+                where_out.append((ci, t0))
+            first += width
+        n_groups = len(where)
+        n_runs = n_groups // RUN
+
+        wgrp = const.tile([P, UNITS, 4], BF16, name="wgrp", align_bytes=64)
+        nc.vector.tensor_copy(out=wgrp[:], in_=wraw[:].rearrange("p t c -> p c t"))
+        wcodes = const.tile([P, UNITS], U32, name="wcodes", align_bytes=64)
+        wscales = const.tile([P, UNITS], U8, name="wscales", align_bytes=64)
+        nc.vector.quantize_mx(
+            out=wcodes[:].bitcast(FP8X4),
+            scales=wscales[:],
+            in_=wgrp[:].rearrange("p c t -> p (c t)"),
+        )
+        bias_sb = const.tile([P, GROUP * UNITS], F32, name="bias_sb")
+
+        banks = {}
+        grouped = {}
+        quantised = {}
+        sums = {}
+
+        def transposes(g):
+            ci, t0 = where[g]
+            words = x_tiles[ci][:].bitcast(F32)
+            for b in range(2):
+                xt = tps.tile([P, 512], F32, name="xt", tag="xt")
+                for j in range(2):
+                    for h in range(2):
+                        col = (t0 + 2 * b + j) * 256
+                        nc.tensor.transpose(
+                            xt[:, 128 * (2 * j + h) : 128 * (2 * j + h) + 128],
+                            words[:, col + h : col + 256 : 2],
+                            ident[:],
+                        )
+                banks[(g, b)] = xt
+
+        def copies(g):
+            grp = stage.tile([P, GROUP * P * 4], BF16, name="grp", tag="grp", align_bytes=64)
+            view = grp[:].bitcast(F32).rearrange("p (j r h) -> p j r h", j=GROUP, h=2)
+            for b in range(2):
+                nc.scalar.copy(
+                    out=view[:, 2 * b : 2 * b + 2, :, :],
+                    in_=banks[(g, b)][:].rearrange("p (j h r) -> p j r h", j=2, h=2),
+                )
+            grouped[g] = grp
+
+        def quantise(g):
+            codes = stage.tile([P, GROUP * P], U32, name="codes", tag="codes", align_bytes=64)
+            scales = stage.tile([P, GROUP * P], U8, name="scales", tag="scales", align_bytes=64)
+            nc.vector.quantize_mx(out=codes[:].bitcast(FP8X4), scales=scales[:], in_=grouped[g][:])
+            quantised[g] = (codes, scales)
+
+        def passes(g):
+            codes, scales = quantised[g]
+            acc = ops.tile([P, GROUP * UNITS], F32, name="acc", tag="acc")
+            for i in range(GROUP):
+                nc.tensor.matmul_mx(
+                    out=acc[:, UNITS * i : UNITS * i + UNITS],
+                    lhsT=codes[:, P * i : P * i + P].bitcast(FP8X4),
+                    lhsT_scale=scales[:, P * i : P * i + P],
+                    rhs=wcodes[:].bitcast(FP8X4),
+                    rhs_scale=wscales[:],
+                    start=True,
+                    stop=True,
+                )
+            sums[g] = acc
+
+        def add_bias(g):
+            ci, t0 = where_out[g]
+            oc, first_tile, width = o_tiles[ci]
+            nc.vector.tensor_tensor(
+                out=oc[:, t0 * UNITS : (t0 + GROUP) * UNITS],
+                in0=sums[g][:],
+                in1=bias_sb[:],
+                op=mybir.AluOpType.add,
+            )
+            if t0 + GROUP == width:
+                nc.sync.dma_start(
+                    out=of[:, first_tile * UNITS : (first_tile + width) * UNITS], in_=oc[:]
+                )
+
+        for s in range(n_runs + 1):
+            if s < n_runs:
+                for i in range(RUN):
+                    transposes(RUN * s + i)
+                for i in range(RUN):
+                    copies(RUN * s + i)
+            if s == 1:
+                bps = ops.tile([P, GROUP * UNITS], F32, name="bps", tag="acc")
+                for i in range(GROUP):
+                    nc.tensor.matmul(
+                        out=bps[:, UNITS * i : UNITS * i + UNITS],
+                        lhsT=ones[:],
+                        rhs=brow[:],
+                        start=True,
+                        stop=True,
+                    )
+                nc.vector.tensor_copy(out=bias_sb[:], in_=bps[:])
+            if s >= 1:
+                for i in range(RUN):
+                    passes(RUN * (s - 1) + i)
+            for i in range(RUN):
+                if s < n_runs:
+                    quantise(RUN * s + i)
+                if s >= 1:
+                    add_bias(RUN * (s - 1) + i)

@@ -85,9 +85,22 @@ def tile_bitlinear_t_kernel(tc, x, kernel, bias, out):
         bias_sb = const.tile([P, GROUP * UNITS], F32, name="bias_sb")
 
         banks = {}
+        halves = {}
         grouped = {}
         quantised = {}
         sums = {}
+
+        def split_words(g):
+            ci, t0 = where[g]
+            words = x_tiles[ci][:].bitcast(F32)
+            half = stage.tile([P, 512], F32, name="half", tag="half", bufs=6)
+            source = words[:, (t0 + 2) * 256 : (t0 + 4) * 256]
+            copy = nc.vector.tensor_copy if g % 2 == 0 else nc.scalar.copy
+            copy(
+                out=half[:].rearrange("p (j h w) -> p j h w", j=2, h=2),
+                in_=source.rearrange("p (j w h) -> p j h w", j=2, h=2),
+            )
+            halves[g] = half
 
         def transposes(g):
             ci, t0 = where[g]
@@ -97,11 +110,12 @@ def tile_bitlinear_t_kernel(tc, x, kernel, bias, out):
                 for j in range(2):
                     for h in range(2):
                         col = (t0 + 2 * b + j) * 256
-                        nc.tensor.transpose(
-                            xt[:, 128 * (2 * j + h) : 128 * (2 * j + h) + 128],
-                            words[:, col + h : col + 256 : 2],
-                            ident[:],
-                        )
+                        side = 128 * (2 * j + h)
+                        if b == 1 and g in halves:
+                            block = halves[g][:, side : side + 128]
+                        else:
+                            block = words[:, col + h : col + 256 : 2]
+                        nc.tensor.transpose(xt[:, side : side + 128], block, ident[:])
                 banks[(g, b)] = xt
 
         def copies(g):
@@ -174,3 +188,6 @@ def tile_bitlinear_t_kernel(tc, x, kernel, bias, out):
                     quantise(RUN * s + i)
                 if s >= 1:
                     add_bias(RUN * (s - 1) + i)
+            if 3 <= s and s + 2 < n_runs:
+                for i in range(RUN):
+                    split_words(RUN * (s + 2) + i)

@@ -20,6 +20,7 @@ FLOPS = 2 * TOKENS * D * UNITS
 LOADS = [4, 4, 8, 16, 16, 16, 16, 16, 16, 16]
 STORES = [64, 32, 16, 8, 8]
 TILES = TOKENS // P
+SPAN = 16
 GROUP = 4
 RUN = 2
 T_BANKS = 5
@@ -28,8 +29,8 @@ O_BANKS = 3
 
 def tile_bitlinear_t_kernel(tc, x, kernel, bias, out):
     nc = tc.nc
-    xf = x.flatten_outer_dims().rearrange("(p t) d -> p (t d)", t=TILES)
-    of = out.flatten_outer_dims().rearrange("(p t) u -> p (t u)", t=TILES)
+    xf = x.flatten_outer_dims().rearrange("(s p t) d -> p s (t d)", p=P, t=SPAN)
+    of = out.flatten_outer_dims().rearrange("(s p t) u -> p s (t u)", p=P, t=SPAN)
     assert sum(LOADS) == TILES and sum(STORES) == TILES
 
     with ExitStack() as ctx:
@@ -56,7 +57,7 @@ def tile_bitlinear_t_kernel(tc, x, kernel, bias, out):
         first = 0
         for ci, width in enumerate(LOADS):
             xc = xin.tile([P, width * D], BF16, name="x%d" % ci)
-            nc.sync.dma_start(out=xc[:], in_=xf[:, first * D : (first + width) * D])
+            nc.sync.dma_start(out=xc[:], in_=xf[:, first // SPAN, first % SPAN * D : (first % SPAN + width) * D])
             x_tiles.append(xc)
             for t0 in range(0, width, GROUP):
                 where.append((ci, t0))
@@ -95,7 +96,7 @@ def tile_bitlinear_t_kernel(tc, x, kernel, bias, out):
             words = x_tiles[ci][:].bitcast(F32)
             half = stage.tile([P, 512], F32, name="half", tag="half", bufs=6)
             source = words[:, (t0 + 2) * 256 : (t0 + 4) * 256]
-            copy = nc.vector.tensor_copy if g % 2 == 0 else nc.scalar.copy
+            copy = nc.vector.tensor_copy if g % 4 == 0 else nc.scalar.copy
             copy(
                 out=half[:].rearrange("p (j h w) -> p j h w", j=2, h=2),
                 in_=source.rearrange("p (j w h) -> p j h w", j=2, h=2),
@@ -159,9 +160,15 @@ def tile_bitlinear_t_kernel(tc, x, kernel, bias, out):
                 op=mybir.AluOpType.add,
             )
             if t0 + GROUP == width:
-                nc.sync.dma_start(
-                    out=of[:, first_tile * UNITS : (first_tile + width) * UNITS], in_=oc[:]
-                )
+                span = first_tile // SPAN
+                if width >= SPAN:
+                    nc.sync.dma_start(
+                        out=of[:, span : span + width // SPAN, :],
+                        in_=oc[:].rearrange("p (s c) -> p s c", c=SPAN * UNITS),
+                    )
+                else:
+                    col = first_tile % SPAN * UNITS
+                    nc.sync.dma_start(out=of[:, span, col : col + width * UNITS], in_=oc[:])
 
         for s in range(n_runs + 1):
             if s < n_runs:
@@ -189,5 +196,4 @@ def tile_bitlinear_t_kernel(tc, x, kernel, bias, out):
                 if s >= 1:
                     add_bias(RUN * (s - 1) + i)
             if 3 <= s and s + 2 < n_runs:
-                for i in range(RUN):
-                    split_words(RUN * (s + 2) + i)
+                split_words(RUN * (s + 2))

@@ -17,10 +17,10 @@ D = 512
 UNITS = 128
 FLOPS = 2 * TOKENS * D * UNITS
 
-LOADS = [4, 4, 8, 16, 16, 16, 16, 16, 16, 16]
+LOADS = [4, 8, 8, 12, 16, 16, 16, 16, 32]
 STORES = [64, 32, 16, 8, 8]
 TILES = TOKENS // P
-SPAN = 16
+SPAN = 32
 GROUP = 4
 RUN = 2
 T_BANKS = 5

from contextlib import ExitStack

import concourse.bass as bass
import concourse.mybir as mybir
import concourse.tile as tile
from concourse.masks import make_identity

F32 = mybir.dt.float32
BF16 = mybir.dt.bfloat16
U32 = mybir.dt.uint32
U8 = mybir.dt.uint8
FP8X4 = mybir.dt.float8_e4m3fn_x4

P = 128
TOKENS = 8 * 2048
D = 512
UNITS = 128
FLOPS = 2 * TOKENS * D * UNITS

LOADS = [4, 8, 8, 12, 16, 16, 16, 16, 32]
STORES = [64, 32, 16, 8, 8]
TILES = TOKENS // P
SPAN = 32
GROUP = 4
RUN = 2
T_BANKS = 5
O_BANKS = 3


def tile_bitlinear_t_kernel(tc, x, kernel, bias, out):
    nc = tc.nc
    xf = x.flatten_outer_dims().rearrange("(s p t) d -> p s (t d)", p=P, t=SPAN)
    of = out.flatten_outer_dims().rearrange("(s p t) u -> p s (t u)", p=P, t=SPAN)
    assert sum(LOADS) == TILES and sum(STORES) == TILES

    with ExitStack() as ctx:
        ctx.enter_context(tc.manual_schedule())
        const = ctx.enter_context(tc.tile_pool(name="const", bufs=1))
        xin = ctx.enter_context(tc.tile_pool(name="xin", bufs=1))
        res = ctx.enter_context(tc.tile_pool(name="res", bufs=1))
        stage = ctx.enter_context(tc.tile_pool(name="stage", bufs=4))
        tps = ctx.enter_context(tc.psum_pool(name="tps", bufs=T_BANKS))
        ops = ctx.enter_context(tc.psum_pool(name="ops", bufs=O_BANKS))

        wraw = const.tile([P, 4, UNITS], BF16, name="wraw")
        nc.scalar.dma_start(out=wraw[:], in_=kernel.rearrange("(p j) c -> p j c", j=4))
        brow = const.tile([P, UNITS], BF16, name="brow")
        nc.vector.memset(brow[:], 0.0)
        nc.scalar.dma_start(out=brow[0:1, :], in_=bias.rearrange("(o u) -> o u", o=1))
        ones = const.tile([P, P], BF16, name="ones")
        nc.vector.memset(ones[:], 1.0)
        ident = const.tile([P, P], F32, name="ident")
        make_identity(nc, ident[:])

        x_tiles = []
        where = []
        first = 0
        for ci, width in enumerate(LOADS):
            xc = xin.tile([P, width * D], BF16, name="x%d" % ci)
            nc.sync.dma_start(out=xc[:], in_=xf[:, first // SPAN, first % SPAN * D : (first % SPAN + width) * D])
            x_tiles.append(xc)
            for t0 in range(0, width, GROUP):
                where.append((ci, t0))
            first += width
        o_tiles = []
        where_out = []
        first = 0
        for ci, width in enumerate(STORES):
            oc = res.tile([P, width * UNITS], F32, name="o%d" % ci)
            o_tiles.append((oc, first, width))
            for t0 in range(0, width, GROUP):
                where_out.append((ci, t0))
            first += width
        n_groups = len(where)
        n_runs = n_groups // RUN

        wgrp = const.tile([P, UNITS, 4], BF16, name="wgrp", align_bytes=64)
        nc.vector.tensor_copy(out=wgrp[:], in_=wraw[:].rearrange("p t c -> p c t"))
        wcodes = const.tile([P, UNITS], U32, name="wcodes", align_bytes=64)
        wscales = const.tile([P, UNITS], U8, name="wscales", align_bytes=64)
        nc.vector.quantize_mx(
            out=wcodes[:].bitcast(FP8X4),
            scales=wscales[:],
            in_=wgrp[:].rearrange("p c t -> p (c t)"),
        )
        bias_sb = const.tile([P, GROUP * UNITS], F32, name="bias_sb")

        banks = {}
        halves = {}
        grouped = {}
        quantised = {}
        sums = {}

        def split_words(g):
            ci, t0 = where[g]
            words = x_tiles[ci][:].bitcast(F32)
            half = stage.tile([P, 512], F32, name="half", tag="half", bufs=6)
            source = words[:, (t0 + 2) * 256 : (t0 + 4) * 256]
            copy = nc.vector.tensor_copy if g % 4 == 0 else nc.scalar.copy
            copy(
                out=half[:].rearrange("p (j h w) -> p j h w", j=2, h=2),
                in_=source.rearrange("p (j w h) -> p j h w", j=2, h=2),
            )
            halves[g] = half

        def transposes(g):
            ci, t0 = where[g]
            words = x_tiles[ci][:].bitcast(F32)
            for b in range(2):
                xt = tps.tile([P, 512], F32, name="xt", tag="xt")
                for j in range(2):
                    for h in range(2):
                        col = (t0 + 2 * b + j) * 256
                        side = 128 * (2 * j + h)
                        if b == 1 and g in halves:
                            block = halves[g][:, side : side + 128]
                        else:
                            block = words[:, col + h : col + 256 : 2]
                        nc.tensor.transpose(xt[:, side : side + 128], block, ident[:])
                banks[(g, b)] = xt

        def copies(g):
            grp = stage.tile([P, GROUP * P * 4], BF16, name="grp", tag="grp", align_bytes=64)
            view = grp[:].bitcast(F32).rearrange("p (j r h) -> p j r h", j=GROUP, h=2)
            for b in range(2):
                nc.scalar.copy(
                    out=view[:, 2 * b : 2 * b + 2, :, :],
                    in_=banks[(g, b)][:].rearrange("p (j h r) -> p j r h", j=2, h=2),
                )
            grouped[g] = grp

        def quantise(g):
            codes = stage.tile([P, GROUP * P], U32, name="codes", tag="codes", align_bytes=64)
            scales = stage.tile([P, GROUP * P], U8, name="scales", tag="scales", align_bytes=64)
            nc.vector.quantize_mx(out=codes[:].bitcast(FP8X4), scales=scales[:], in_=grouped[g][:])
            quantised[g] = (codes, scales)

        def passes(g):
            codes, scales = quantised[g]
            acc = ops.tile([P, GROUP * UNITS], F32, name="acc", tag="acc")
            for i in range(GROUP):
                nc.tensor.matmul_mx(
                    out=acc[:, UNITS * i : UNITS * i + UNITS],
                    lhsT=codes[:, P * i : P * i + P].bitcast(FP8X4),
                    lhsT_scale=scales[:, P * i : P * i + P],
                    rhs=wcodes[:].bitcast(FP8X4),
                    rhs_scale=wscales[:],
                    start=True,
                    stop=True,
                )
            sums[g] = acc

        def add_bias(g):
            ci, t0 = where_out[g]
            oc, first_tile, width = o_tiles[ci]
            nc.vector.tensor_tensor(
                out=oc[:, t0 * UNITS : (t0 + GROUP) * UNITS],
                in0=sums[g][:],
                in1=bias_sb[:],
                op=mybir.AluOpType.add,
            )
            if t0 + GROUP == width:
                span = first_tile // SPAN
                if width >= SPAN:
                    nc.sync.dma_start(
                        out=of[:, span : span + width // SPAN, :],
                        in_=oc[:].rearrange("p (s c) -> p s c", c=SPAN * UNITS),
                    )
                else:
                    col = first_tile % SPAN * UNITS
                    nc.sync.dma_start(out=of[:, span, col : col + width * UNITS], in_=oc[:])

        for s in range(n_runs + 1):
            if s < n_runs:
                for i in range(RUN):
                    transposes(RUN * s + i)
                for i in range(RUN):
                    copies(RUN * s + i)
            if s == 1:
                bps = ops.tile([P, GROUP * UNITS], F32, name="bps", tag="acc")
                for i in range(GROUP):
                    nc.tensor.matmul(
                        out=bps[:, UNITS * i : UNITS * i + UNITS],
                        lhsT=ones[:],
                        rhs=brow[:],
                        start=True,
                        stop=True,
                    )
                nc.vector.tensor_copy(out=bias_sb[:], in_=bps[:])
            if s >= 1:
                for i in range(RUN):
                    passes(RUN * (s - 1) + i)
            for i in range(RUN):
                if s < n_runs:
                    quantise(RUN * s + i)
                if s >= 1:
                    add_bias(RUN * (s - 1) + i)
            if 3 <= s and s + 2 < n_runs:
                split_words(RUN * (s + 2))
